import numpy as np
import ml_dtypes


def mxq(x, axis, fmt="e4m3"):
    dtype, down = {"e4m3": (ml_dtypes.float8_e4m3fn, 7), "e5m2": (ml_dtypes.float8_e5m2, 14)}[fmt]
    v = np.moveaxis(np.asarray(x, np.float32).astype(ml_dtypes.bfloat16).astype(np.float64), axis, -1)
    blocks = v.reshape(v.shape[:-1] + (-1, 32))
    amax = np.abs(blocks).max(-1, keepdims=True)
    byte = np.maximum(np.where(amax > 0, np.frexp(amax)[1] - 1 + 127, 0) - down, 1)
    scale = np.exp2(byte - 127.0)
    codes = (blocks / scale).astype(np.float32).astype(dtype).astype(np.float64)
    return np.moveaxis((codes * scale).reshape(v.shape), -1, axis)


WIDE = False


def mx_kscale(k):
    if not WIDE:
        return np.ones(k)
    levels = np.array([10, -10, 5, -5, 0])
    a = np.random.permutation(np.resize(levels, k // 512 * 4)).reshape(k // 512, 4)
    idx = np.arange(k)
    return np.exp2(a[idx // 512, idx % 128 // 32])


BF16 = ml_dtypes.bfloat16


def bf(x):
    return np.asarray(x, np.float32).astype(BF16)


def f64(x):
    return np.asarray(x).astype(np.float64)


N, MUL, RANK, D0, D1, D2 = 128, 1536, 128, 1, 3, 5
DIMS = (D0, D1, D2)
SD = D0 + D1 + D2
NI = len(DIMS)
SCALING = 2.0


def setup_inputs():
    s = mx_kscale(MUL)
    return {"x": bf(np.random.standard_normal((N, SD * MUL)) * np.tile(s, SD)),
            "a_lora": bf(np.random.standard_normal((N, SD * RANK)) * 0.5),
            "w_base": bf(np.random.standard_normal((NI, MUL, MUL)) / s[None, :, None]),
            "w_lora_b": bf(np.random.standard_normal((NI, RANK, MUL)))}


def reference(x, a_lora, w_base, w_lora_b):
    x, a_lora, w_base, w_lora_b = f64(x), f64(a_lora), f64(w_base), f64(w_lora_b)
    pw_base = 1.0 / np.sqrt(MUL)
    pw_b = 1.0 / np.sqrt(RANK)
    n = x.shape[0]
    outs = []
    off = 0
    offa = 0
    for k, d in enumerate(DIMS):
        seg = x[:, off:off + d * MUL].reshape(n * d, MUL)
        y = pw_base * (mxq(seg, 1, "e4m3") @ mxq(w_base[k], 0, "e4m3"))
        a = a_lora[:, offa:offa + d * RANK].reshape(n * d, RANK)
        b = pw_b * (a @ w_lora_b[k])
        outs.append((y + SCALING * b).reshape(n, d * MUL))
        off += d * MUL
        offa += d * RANK
    return np.concatenate(outs, axis=-1)

@@ -1,0 +1,189 @@
+import math
+from contextlib import ExitStack
+
+import concourse.mybir as mybir
+from concourse.masks import make_identity
+
+F32 = mybir.dt.float32
+BF16 = mybir.dt.bfloat16
+U32 = mybir.dt.uint32
+U8 = mybir.dt.uint8
+FP8X4 = mybir.dt.float8_e4m3fn_x4
+MULT = mybir.AluOpType.mult
+ADD = mybir.AluOpType.add
+
+P = 128
+PACK = 4
+K_PASS = P * PACK
+N_TILE = 512
+
+NODES = 128
+MUL = 1536
+RANK = 128
+COMPONENTS = (1, 3, 5)
+FIRST_BLOCK = (0, 1, 4)
+BLOCKS = sum(COMPONENTS)
+PASSES = MUL // K_PASS
+COL_TILES = MUL // N_TILE
+WORDS_PASS = K_PASS // 2
+
+IRREP_ORDER = (2, 1, 0)
+
+BASE_FACTOR = 1.0 / math.sqrt(MUL)
+LORA_FACTOR = 2.0 / math.sqrt(RANK)
+
+VECTOR_COLS = N_TILE // 2
+
+FLOPS = 2 * NODES * BLOCKS * MUL * (MUL + RANK)
+
+
+def regrouped(rows, grouped):
+    return (
+        grouped.rearrange("p (c i) t -> p c t i", i=4),
+        rows.rearrange("p t (c i) -> p c t i", i=4),
+    )
+
+
+def tile_loracuetlinear_pa_kernel(tc, x, a_lora, w_base, w_lora_b, out):
+    nc = tc.nc
+    with ExitStack() as ctx:
+        resident = ctx.enter_context(tc.tile_pool(name="resident", bufs=1))
+        raw_pool = ctx.enter_context(tc.tile_pool(name="raw", bufs=5))
+        grouped_pool = ctx.enter_context(tc.tile_pool(name="grouped", bufs=4))
+        x_grouped_pool = ctx.enter_context(tc.tile_pool(name="x_grouped", bufs=3))
+        codes_pool = ctx.enter_context(tc.tile_pool(name="codes", bufs=2))
+        out_pool = ctx.enter_context(tc.tile_pool(name="out", bufs=6))
+        transposed_pool = ctx.enter_context(tc.psum_pool(name="transposed", bufs=2))
+        lora_pool = ctx.enter_context(tc.psum_pool(name="lora", bufs=2))
+        acc_pool = ctx.enter_context(tc.psum_pool(name="acc", bufs=4))
+
+        ident_f32 = resident.tile([P, P], F32)
+        make_identity(nc, ident_f32[:])
+        ident_bf16 = resident.tile([P, P], BF16)
+        make_identity(nc, ident_bf16[:])
+
+        w_raw = {}
+        a_raw = {}
+        lora_w = {}
+        x_raw = {}
+
+        def load_weight_pass(k, g):
+            raw = raw_pool.tile([P, PACK, MUL], BF16)
+            rows = w_base[k, g * K_PASS : (g + 1) * K_PASS, :]
+            nc.sync.dma_start(out=raw[:], in_=rows.rearrange("(p t) c -> p t c", t=PACK))
+            w_raw[(k, g)] = raw
+
+        for k in IRREP_ORDER:
+            blocks = COMPONENTS[k]
+            first = FIRST_BLOCK[k]
+            load_weight_pass(k, 0)
+            a_raw[k] = resident.tile([P, blocks * RANK], BF16, name="a_raw%d" % k)
+            nc.sync.dma_start(
+                out=a_raw[k][:], in_=a_lora[:, first * RANK : (first + blocks) * RANK]
+            )
+            lora_w[k] = resident.tile([P, MUL], BF16, name="lora_w%d" % k)
+            nc.sync.dma_start(out=lora_w[k][:], in_=w_lora_b[k, :, :])
+            load_weight_pass(k, 1)
+            x_raw[k] = resident.tile([P, blocks * MUL], BF16, name="x_raw%d" % k)
+            nc.sync.dma_start(
+                out=x_raw[k][:], in_=x[:, first * MUL : (first + blocks) * MUL]
+            )
+            load_weight_pass(k, 2)
+
+        x_codes = resident.tile([P, BLOCKS * PASSES * NODES], U32, align_bytes=64)
+        x_scales = resident.tile([P, BLOCKS * PASSES * NODES], U8, align_bytes=64)
+
+        for k in IRREP_ORDER:
+            blocks = COMPONENTS[k]
+            first = FIRST_BLOCK[k]
+
+            w_codes = codes_pool.tile([P, PASSES, MUL], U32, align_bytes=64)
+            w_scales = codes_pool.tile([P, PASSES, MUL], U8, align_bytes=64)
+            for g in range(PASSES):
+                for c in range(COL_TILES):
+                    cols = slice(c * N_TILE, (c + 1) * N_TILE)
+                    split = c * N_TILE + VECTOR_COLS
+                    grouped = grouped_pool.tile([P, N_TILE, PACK], BF16, align_bytes=64)
+                    to_view, from_view = regrouped(
+                        w_raw[(k, g)][:, :, c * N_TILE : split], grouped[:, :VECTOR_COLS, :]
+                    )
+                    nc.vector.tensor_copy(out=to_view, in_=from_view)
+                    to_view, from_view = regrouped(
+                        w_raw[(k, g)][:, :, split : (c + 1) * N_TILE],
+                        grouped[:, VECTOR_COLS:, :],
+                    )
+                    nc.scalar.copy(out=to_view, in_=from_view)
+                    nc.vector.quantize_mx(
+                        out=w_codes[:, g, cols].bitcast(FP8X4),
+                        scales=w_scales[:, g, cols],
+                        in_=grouped[:].rearrange("p c t -> p (c t)"),
+                    )
+
+            words = x_raw[k][:].bitcast(F32)
+            x_passes = blocks * PASSES
+            for q in range(0, x_passes, 2):
+                n = min(2, x_passes - q)
+                x_t = transposed_pool.tile([P, 2, 2, NODES], F32, tag="transposed")
+                for i in range(n):
+                    pass_words = words[:, (q + i) * WORDS_PASS : (q + i + 1) * WORDS_PASS]
+                    halves = pass_words.rearrange("n (p u) -> n u p", u=2)
+                    for u in range(2):
+                        nc.tensor.transpose(x_t[:, i, u, :], halves[:, u, :], ident_f32[:])
+                x_grouped = x_grouped_pool.tile([P, 2 * NODES * PACK], BF16, align_bytes=64)
+                filled = x_grouped[:, : n * NODES * PACK]
+                nc.scalar.copy(
+                    out=filled.bitcast(F32).rearrange("p (i m u) -> p i m u", i=n, u=2),
+                    in_=x_t[:, :n, :, :].rearrange("p i u m -> p i m u"),
+                )
+                at = (first * PASSES + q) * NODES
+                nc.vector.quantize_mx(
+                    out=x_codes[:, at : at + n * NODES].bitcast(FP8X4),
+                    scales=x_scales[:, at : at + n * NODES],
+                    in_=filled,
+                )
+
+            a_t_psum = transposed_pool.tile([P, blocks, NODES], BF16, tag="transposed")
+            for i in range(blocks):
+                nc.tensor.transpose(
+                    a_t_psum[:, i, :], a_raw[k][:, i * RANK : (i + 1) * RANK], ident_bf16[:]
+                )
+            a_t = resident.tile([P, blocks, NODES], BF16, name="a_t%d" % k)
+            nc.scalar.copy(out=a_t[:], in_=a_t_psum[:])
+
+            for i in range(blocks):
+                j = first + i
+                out_sb = out_pool.tile([P, MUL], F32)
+                for c in range(COL_TILES):
+                    cols = slice(c * N_TILE, (c + 1) * N_TILE)
+                    lora_psum = lora_pool.tile([P, N_TILE], F32)
+                    nc.tensor.matmul(
+                        out=lora_psum[:],
+                        lhsT=a_t[:, i, :],
+                        rhs=lora_w[k][:, cols],
+                        start=True,
+                        stop=True,
+                    )
+                    nc.scalar.mul(out=out_sb[:, cols], in_=lora_psum[:], mul=LORA_FACTOR)
+                for c in range(COL_TILES):
+                    cols = slice(c * N_TILE, (c + 1) * N_TILE)
+                    acc = acc_pool.tile([P, N_TILE], F32)
+                    for g in range(PASSES):
+                        at = (j * PASSES + g) * NODES
+                        nc.tensor.matmul_mx(
+                            out=acc[:],
+                            lhsT=x_codes[:, at : at + NODES].bitcast(FP8X4),
+                            lhsT_scale=x_scales[:, at : at + NODES],
+                            rhs=w_codes[:, g, cols].bitcast(FP8X4),
+                            rhs_scale=w_scales[:, g, cols],
+                            start=(g == 0),
+                            stop=(g == PASSES - 1),
+                        )
+                    nc.vector.scalar_tensor_tensor(
+                        out=out_sb[:, cols],
+                        in0=acc[:],
+                        scalar=BASE_FACTOR,
+                        in1=out_sb[:, cols],
+                        op0=MULT,
+                        op1=ADD,
+                    )
+                nc.gpsimd.dma_start(out=out[:, j * MUL : (j + 1) * MUL], in_=out_sb[:])

@@ -54,8 +54,7 @@ def tile_loracuetlinear_pa_kernel(tc, x, a_lora, w_base, w_lora_b, out):
         codes_pool = ctx.enter_context(tc.tile_pool(name="codes", bufs=2))
         out_pool = ctx.enter_context(tc.tile_pool(name="out", bufs=6))
         transposed_pool = ctx.enter_context(tc.psum_pool(name="transposed", bufs=2))
-        lora_pool = ctx.enter_context(tc.psum_pool(name="lora", bufs=2))
-        acc_pool = ctx.enter_context(tc.psum_pool(name="acc", bufs=4))
+        product_pool = ctx.enter_context(tc.psum_pool(name="product", bufs=6))
 
         ident_f32 = resident.tile([P, P], F32)
         make_identity(nc, ident_f32[:])
@@ -97,27 +96,13 @@ def tile_loracuetlinear_pa_kernel(tc, x, a_lora, w_base, w_lora_b, out):
             blocks = COMPONENTS[k]
             first = FIRST_BLOCK[k]
 
-            w_codes = codes_pool.tile([P, PASSES, MUL], U32, align_bytes=64)
-            w_scales = codes_pool.tile([P, PASSES, MUL], U8, align_bytes=64)
-            for g in range(PASSES):
-                for c in range(COL_TILES):
-                    cols = slice(c * N_TILE, (c + 1) * N_TILE)
-                    split = c * N_TILE + VECTOR_COLS
-                    grouped = grouped_pool.tile([P, N_TILE, PACK], BF16, align_bytes=64)
-                    to_view, from_view = regrouped(
-                        w_raw[(k, g)][:, :, c * N_TILE : split], grouped[:, :VECTOR_COLS, :]
-                    )
-                    nc.vector.tensor_copy(out=to_view, in_=from_view)
-                    to_view, from_view = regrouped(
-                        w_raw[(k, g)][:, :, split : (c + 1) * N_TILE],
-                        grouped[:, VECTOR_COLS:, :],
-                    )
-                    nc.scalar.copy(out=to_view, in_=from_view)
-                    nc.vector.quantize_mx(
-                        out=w_codes[:, g, cols].bitcast(FP8X4),
-                        scales=w_scales[:, g, cols],
-                        in_=grouped[:].rearrange("p c t -> p (c t)"),
-                    )
+            a_t_psum = transposed_pool.tile([P, blocks, NODES], BF16, tag="transposed")
+            for i in range(blocks):
+                nc.tensor.transpose(
+                    a_t_psum[:, i, :], a_raw[k][:, i * RANK : (i + 1) * RANK], ident_bf16[:]
+                )
+            a_t = resident.tile([P, blocks, NODES], BF16, name="a_t%d" % k)
+            nc.scalar.copy(out=a_t[:], in_=a_t_psum[:])
 
             words = x_raw[k][:].bitcast(F32)
             x_passes = blocks * PASSES
@@ -142,20 +127,34 @@ def tile_loracuetlinear_pa_kernel(tc, x, a_lora, w_base, w_lora_b, out):
                     in_=filled,
                 )
 
-            a_t_psum = transposed_pool.tile([P, blocks, NODES], BF16, tag="transposed")
-            for i in range(blocks):
-                nc.tensor.transpose(
-                    a_t_psum[:, i, :], a_raw[k][:, i * RANK : (i + 1) * RANK], ident_bf16[:]
-                )
-            a_t = resident.tile([P, blocks, NODES], BF16, name="a_t%d" % k)
-            nc.scalar.copy(out=a_t[:], in_=a_t_psum[:])
+            w_codes = codes_pool.tile([P, PASSES, MUL], U32, align_bytes=64)
+            w_scales = codes_pool.tile([P, PASSES, MUL], U8, align_bytes=64)
+            for g in range(PASSES):
+                for c in range(COL_TILES):
+                    cols = slice(c * N_TILE, (c + 1) * N_TILE)
+                    split = c * N_TILE + VECTOR_COLS
+                    grouped = grouped_pool.tile([P, N_TILE, PACK], BF16, align_bytes=64)
+                    to_view, from_view = regrouped(
+                        w_raw[(k, g)][:, :, c * N_TILE : split], grouped[:, :VECTOR_COLS, :]
+                    )
+                    nc.vector.tensor_copy(out=to_view, in_=from_view)
+                    to_view, from_view = regrouped(
+                        w_raw[(k, g)][:, :, split : (c + 1) * N_TILE],
+                        grouped[:, VECTOR_COLS:, :],
+                    )
+                    nc.scalar.copy(out=to_view, in_=from_view)
+                    nc.vector.quantize_mx(
+                        out=w_codes[:, g, cols].bitcast(FP8X4),
+                        scales=w_scales[:, g, cols],
+                        in_=grouped[:].rearrange("p c t -> p (c t)"),
+                    )
 
             for i in range(blocks):
                 j = first + i
                 out_sb = out_pool.tile([P, MUL], F32)
                 for c in range(COL_TILES):
                     cols = slice(c * N_TILE, (c + 1) * N_TILE)
-                    lora_psum = lora_pool.tile([P, N_TILE], F32)
+                    lora_psum = product_pool.tile([P, N_TILE], F32, tag="product")
                     nc.tensor.matmul(
                         out=lora_psum[:],
                         lhsT=a_t[:, i, :],
@@ -166,7 +165,7 @@ def tile_loracuetlinear_pa_kernel(tc, x, a_lora, w_base, w_lora_b, out):
                     nc.scalar.mul(out=out_sb[:, cols], in_=lora_psum[:], mul=LORA_FACTOR)
                 for c in range(COL_TILES):
                     cols = slice(c * N_TILE, (c + 1) * N_TILE)
-                    acc = acc_pool.tile([P, N_TILE], F32)
+                    acc = product_pool.tile([P, N_TILE], F32, tag="product")
                     for g in range(PASSES):
                         at = (j * PASSES + g) * NODES
                         nc.tensor.matmul_mx(
@@ -186,4 +185,7 @@ def tile_loracuetlinear_pa_kernel(tc, x, a_lora, w_base, w_lora_b, out):
                         op0=MULT,
                         op1=ADD,
                     )
-                nc.gpsimd.dma_start(out=out[:, j * MUL : (j + 1) * MUL], in_=out_sb[:])
+                    nc.sync.dma_start(
+                        out=out[:, j * MUL + c * N_TILE : j * MUL + (c + 1) * N_TILE],
+                        in_=out_sb[:, cols],
+                    )

@@ -32,7 +32,7 @@ IRREP_ORDER = (2, 1, 0)
 BASE_FACTOR = 1.0 / math.sqrt(MUL)
 LORA_FACTOR = 2.0 / math.sqrt(RANK)
 
-VECTOR_COLS = N_TILE // 2
+VECTOR_COLS = (N_TILE, 144, 144)
 
 FLOPS = 2 * NODES * BLOCKS * MUL * (MUL + RANK)
 
@@ -48,11 +48,10 @@ def tile_loracuetlinear_pa_kernel(tc, x, a_lora, w_base, w_lora_b, out):
     nc = tc.nc
     with ExitStack() as ctx:
         resident = ctx.enter_context(tc.tile_pool(name="resident", bufs=1))
-        raw_pool = ctx.enter_context(tc.tile_pool(name="raw", bufs=5))
+        raw_pool = ctx.enter_context(tc.tile_pool(name="raw", bufs=4))
         grouped_pool = ctx.enter_context(tc.tile_pool(name="grouped", bufs=4))
         x_grouped_pool = ctx.enter_context(tc.tile_pool(name="x_grouped", bufs=3))
         codes_pool = ctx.enter_context(tc.tile_pool(name="codes", bufs=2))
-        out_pool = ctx.enter_context(tc.tile_pool(name="out", bufs=6))
         transposed_pool = ctx.enter_context(tc.psum_pool(name="transposed", bufs=2))
         product_pool = ctx.enter_context(tc.psum_pool(name="product", bufs=6))
 
@@ -61,49 +60,89 @@ def tile_loracuetlinear_pa_kernel(tc, x, a_lora, w_base, w_lora_b, out):
         ident_bf16 = resident.tile([P, P], BF16)
         make_identity(nc, ident_bf16[:])
 
-        w_raw = {}
-        a_raw = {}
+        a_raw = resident.tile([P, BLOCKS * RANK], BF16)
+        nc.sync.dma_start(out=a_raw[:], in_=a_lora[:, :])
+
         lora_w = {}
         x_raw = {}
-
-        def load_weight_pass(k, g):
-            raw = raw_pool.tile([P, PACK, MUL], BF16)
-            rows = w_base[k, g * K_PASS : (g + 1) * K_PASS, :]
-            nc.sync.dma_start(out=raw[:], in_=rows.rearrange("(p t) c -> p t c", t=PACK))
-            w_raw[(k, g)] = raw
-
+        side_loads = []
         for k in IRREP_ORDER:
-            blocks = COMPONENTS[k]
-            first = FIRST_BLOCK[k]
-            load_weight_pass(k, 0)
-            a_raw[k] = resident.tile([P, blocks * RANK], BF16, name="a_raw%d" % k)
-            nc.sync.dma_start(
-                out=a_raw[k][:], in_=a_lora[:, first * RANK : (first + blocks) * RANK]
-            )
             lora_w[k] = resident.tile([P, MUL], BF16, name="lora_w%d" % k)
-            nc.sync.dma_start(out=lora_w[k][:], in_=w_lora_b[k, :, :])
-            load_weight_pass(k, 1)
+            side_loads.append((lora_w[k], w_lora_b[k, :, :]))
+        for k in IRREP_ORDER:
+            first, blocks = FIRST_BLOCK[k], COMPONENTS[k]
             x_raw[k] = resident.tile([P, blocks * MUL], BF16, name="x_raw%d" % k)
+            side_loads.append((x_raw[k], x[:, first * MUL : (first + blocks) * MUL]))
+
+        w_raw = {}
+        for n, (k, g) in enumerate([(k, g) for k in IRREP_ORDER for g in range(PASSES)]):
+            if n < len(side_loads):
+                side_tile, side_source = side_loads[n]
+                nc.sync.dma_start(out=side_tile[:], in_=side_source)
+            w_raw[(k, g)] = raw_pool.tile([P, PACK, MUL], BF16, name="w_raw")
+            rows = w_base[k, g * K_PASS : (g + 1) * K_PASS, :]
             nc.sync.dma_start(
-                out=x_raw[k][:], in_=x[:, first * MUL : (first + blocks) * MUL]
+                out=w_raw[(k, g)][:], in_=rows.rearrange("(p t) c -> p t c", t=PACK)
             )
-            load_weight_pass(k, 2)
 
         x_codes = resident.tile([P, BLOCKS * PASSES * NODES], U32, align_bytes=64)
         x_scales = resident.tile([P, BLOCKS * PASSES * NODES], U8, align_bytes=64)
+        w_codes = {}
+        w_scales = {}
+        out_sb = [resident.tile([P, MUL], F32, name="out_sb%d" % j) for j in range(BLOCKS)]
 
-        for k in IRREP_ORDER:
-            blocks = COMPONENTS[k]
-            first = FIRST_BLOCK[k]
+        def quantise_weights(k):
+            vector_cols = VECTOR_COLS[IRREP_ORDER.index(k)]
+            w_codes[k] = codes_pool.tile([P, PASSES, MUL], U32, align_bytes=64, name="w_codes")
+            w_scales[k] = codes_pool.tile([P, PASSES, MUL], U8, align_bytes=64, name="w_scales")
+            for g in range(PASSES):
+                for c in range(COL_TILES):
+                    cols = slice(c * N_TILE, (c + 1) * N_TILE)
+                    split = c * N_TILE + vector_cols
+                    grouped = grouped_pool.tile([P, N_TILE, PACK], BF16, align_bytes=64)
+                    to_view, from_view = regrouped(
+                        w_raw[(k, g)][:, :, c * N_TILE : split], grouped[:, :vector_cols, :]
+                    )
+                    nc.vector.tensor_copy(out=to_view, in_=from_view)
+                    if vector_cols < N_TILE:
+                        to_view, from_view = regrouped(
+                            w_raw[(k, g)][:, :, split : (c + 1) * N_TILE],
+                            grouped[:, vector_cols:, :],
+                        )
+                        nc.scalar.copy(out=to_view, in_=from_view)
+                    nc.vector.quantize_mx(
+                        out=w_codes[k][:, g, cols].bitcast(FP8X4),
+                        scales=w_scales[k][:, g, cols],
+                        in_=grouped[:].rearrange("p c t -> p (c t)"),
+                    )
 
+        def lora_products(k):
+            first, blocks = FIRST_BLOCK[k], COMPONENTS[k]
             a_t_psum = transposed_pool.tile([P, blocks, NODES], BF16, tag="transposed")
             for i in range(blocks):
+                j = first + i
                 nc.tensor.transpose(
-                    a_t_psum[:, i, :], a_raw[k][:, i * RANK : (i + 1) * RANK], ident_bf16[:]
+                    a_t_psum[:, i, :], a_raw[:, j * RANK : (j + 1) * RANK], ident_bf16[:]
                 )
             a_t = resident.tile([P, blocks, NODES], BF16, name="a_t%d" % k)
             nc.scalar.copy(out=a_t[:], in_=a_t_psum[:])
+            for i in range(blocks):
+                for c in range(COL_TILES):
+                    cols = slice(c * N_TILE, (c + 1) * N_TILE)
+                    lora_psum = product_pool.tile([P, N_TILE], F32, tag="product")
+                    nc.tensor.matmul(
+                        out=lora_psum[:],
+                        lhsT=a_t[:, i, :],
+                        rhs=lora_w[k][:, cols],
+                        start=True,
+                        stop=True,
+                    )
+                    nc.scalar.mul(
+                        out=out_sb[first + i][:, cols], in_=lora_psum[:], mul=LORA_FACTOR
+                    )
 
+        def quantise_x(k):
+            first, blocks = FIRST_BLOCK[k], COMPONENTS[k]
             words = x_raw[k][:].bitcast(F32)
             x_passes = blocks * PASSES
             for q in range(0, x_passes, 2):
@@ -127,42 +166,9 @@ def tile_loracuetlinear_pa_kernel(tc, x, a_lora, w_base, w_lora_b, out):
                     in_=filled,
                 )
 
-            w_codes = codes_pool.tile([P, PASSES, MUL], U32, align_bytes=64)
-            w_scales = codes_pool.tile([P, PASSES, MUL], U8, align_bytes=64)
-            for g in range(PASSES):
-                for c in range(COL_TILES):
-                    cols = slice(c * N_TILE, (c + 1) * N_TILE)
-                    split = c * N_TILE + VECTOR_COLS
-                    grouped = grouped_pool.tile([P, N_TILE, PACK], BF16, align_bytes=64)
-                    to_view, from_view = regrouped(
-                        w_raw[(k, g)][:, :, c * N_TILE : split], grouped[:, :VECTOR_COLS, :]
-                    )
-                    nc.vector.tensor_copy(out=to_view, in_=from_view)
-                    to_view, from_view = regrouped(
-                        w_raw[(k, g)][:, :, split : (c + 1) * N_TILE],
-                        grouped[:, VECTOR_COLS:, :],
-                    )
-                    nc.scalar.copy(out=to_view, in_=from_view)
-                    nc.vector.quantize_mx(
-                        out=w_codes[:, g, cols].bitcast(FP8X4),
-                        scales=w_scales[:, g, cols],
-                        in_=grouped[:].rearrange("p c t -> p (c t)"),
-                    )
-
-            for i in range(blocks):
-                j = first + i
-                out_sb = out_pool.tile([P, MUL], F32)
-                for c in range(COL_TILES):
-                    cols = slice(c * N_TILE, (c + 1) * N_TILE)
-                    lora_psum = product_pool.tile([P, N_TILE], F32, tag="product")
-                    nc.tensor.matmul(
-                        out=lora_psum[:],
-                        lhsT=a_t[:, i, :],
-                        rhs=lora_w[k][:, cols],
-                        start=True,
-                        stop=True,
-                    )
-                    nc.scalar.mul(out=out_sb[:, cols], in_=lora_psum[:], mul=LORA_FACTOR)
+        def finish_blocks(k):
+            for i in range(COMPONENTS[k]):
+                j = FIRST_BLOCK[k] + i
                 for c in range(COL_TILES):
                     cols = slice(c * N_TILE, (c + 1) * N_TILE)
                     acc = product_pool.tile([P, N_TILE], F32, tag="product")
@@ -172,20 +178,33 @@ def tile_loracuetlinear_pa_kernel(tc, x, a_lora, w_base, w_lora_b, out):
                             out=acc[:],
                             lhsT=x_codes[:, at : at + NODES].bitcast(FP8X4),
                             lhsT_scale=x_scales[:, at : at + NODES],
-                            rhs=w_codes[:, g, cols].bitcast(FP8X4),
-                            rhs_scale=w_scales[:, g, cols],
+                            rhs=w_codes[k][:, g, cols].bitcast(FP8X4),
+                            rhs_scale=w_scales[k][:, g, cols],
                             start=(g == 0),
                             stop=(g == PASSES - 1),
                         )
                     nc.vector.scalar_tensor_tensor(
-                        out=out_sb[:, cols],
+                        out=out_sb[j][:, cols],
                         in0=acc[:],
                         scalar=BASE_FACTOR,
-                        in1=out_sb[:, cols],
+                        in1=out_sb[j][:, cols],
                         op0=MULT,
                         op1=ADD,
                     )
                     nc.sync.dma_start(
                         out=out[:, j * MUL + c * N_TILE : j * MUL + (c + 1) * N_TILE],
-                        in_=out_sb[:, cols],
+                        in_=out_sb[j][:, cols],
                     )
+
+        first_irrep, second_irrep, last_irrep = IRREP_ORDER
+        quantise_weights(first_irrep)
+        for k in IRREP_ORDER:
+            lora_products(k)
+        quantise_x(first_irrep)
+        quantise_weights(second_irrep)
+        finish_blocks(first_irrep)
+        quantise_x(second_irrep)
+        quantise_x(last_irrep)
+        quantise_weights(last_irrep)
+        finish_blocks(second_irrep)
+        finish_blocks(last_irrep)

@@ -32,7 +32,9 @@ IRREP_ORDER = (2, 1, 0)
 BASE_FACTOR = 1.0 / math.sqrt(MUL)
 LORA_FACTOR = 2.0 / math.sqrt(RANK)
 
-VECTOR_COLS = (N_TILE, 144, 144)
+VECTOR_COLS = (N_TILE, 176, 176)
+HEAD_PIECES = 2
+HEAD_VECTOR_COLS = 336
 
 FLOPS = 2 * NODES * BLOCKS * MUL * (MUL + RANK)
 
@@ -49,7 +51,7 @@ def tile_loracuetlinear_pa_kernel(tc, x, a_lora, w_base, w_lora_b, out):
     with ExitStack() as ctx:
         resident = ctx.enter_context(tc.tile_pool(name="resident", bufs=1))
         raw_pool = ctx.enter_context(tc.tile_pool(name="raw", bufs=4))
-        grouped_pool = ctx.enter_context(tc.tile_pool(name="grouped", bufs=4))
+        grouped_pool = ctx.enter_context(tc.tile_pool(name="grouped", bufs=6))
         x_grouped_pool = ctx.enter_context(tc.tile_pool(name="x_grouped", bufs=3))
         codes_pool = ctx.enter_context(tc.tile_pool(name="codes", bufs=2))
         transposed_pool = ctx.enter_context(tc.psum_pool(name="transposed", bufs=2))
@@ -61,7 +63,6 @@ def tile_loracuetlinear_pa_kernel(tc, x, a_lora, w_base, w_lora_b, out):
         make_identity(nc, ident_bf16[:])
 
         a_raw = resident.tile([P, BLOCKS * RANK], BF16)
-        nc.sync.dma_start(out=a_raw[:], in_=a_lora[:, :])
 
         lora_w = {}
         x_raw = {}
@@ -74,16 +75,30 @@ def tile_loracuetlinear_pa_kernel(tc, x, a_lora, w_base, w_lora_b, out):
             x_raw[k] = resident.tile([P, blocks * MUL], BF16, name="x_raw%d" % k)
             side_loads.append((x_raw[k], x[:, first * MUL : (first + blocks) * MUL]))
 
-        w_raw = {}
+        w_piece = {}
         for n, (k, g) in enumerate([(k, g) for k in IRREP_ORDER for g in range(PASSES)]):
-            if n < len(side_loads):
-                side_tile, side_source = side_loads[n]
-                nc.sync.dma_start(out=side_tile[:], in_=side_source)
-            w_raw[(k, g)] = raw_pool.tile([P, PACK, MUL], BF16, name="w_raw")
-            rows = w_base[k, g * K_PASS : (g + 1) * K_PASS, :]
-            nc.sync.dma_start(
-                out=w_raw[(k, g)][:], in_=rows.rearrange("(p t) c -> p t c", t=PACK)
-            )
+            rows = w_base[k, g * K_PASS : (g + 1) * K_PASS, :].rearrange("(p t) c -> p t c", t=PACK)
+            if n == 0:
+                for c in range(COL_TILES):
+                    if c == HEAD_PIECES:
+                        nc.sync.dma_start(out=a_raw[:], in_=a_lora[:, :])
+                        side_tile, side_source = side_loads[0]
+                        nc.sync.dma_start(out=side_tile[:], in_=side_source)
+                    first_raw = grouped_pool.tile(
+                        [P, PACK, N_TILE], BF16, align_bytes=64, tag="grouped"
+                    )
+                    nc.sync.dma_start(
+                        out=first_raw[:], in_=rows[:, :, c * N_TILE : (c + 1) * N_TILE]
+                    )
+                    w_piece[(k, g, c)] = first_raw[:]
+            else:
+                if n < len(side_loads):
+                    side_tile, side_source = side_loads[n]
+                    nc.sync.dma_start(out=side_tile[:], in_=side_source)
+                w_raw = raw_pool.tile([P, PACK, MUL], BF16)
+                nc.sync.dma_start(out=w_raw[:], in_=rows)
+                for c in range(COL_TILES):
+                    w_piece[(k, g, c)] = w_raw[:, :, c * N_TILE : (c + 1) * N_TILE]
 
         x_codes = resident.tile([P, BLOCKS * PASSES * NODES], U32, align_bytes=64)
         x_scales = resident.tile([P, BLOCKS * PASSES * NODES], U8, align_bytes=64)
@@ -92,21 +107,25 @@ def tile_loracuetlinear_pa_kernel(tc, x, a_lora, w_base, w_lora_b, out):
         out_sb = [resident.tile([P, MUL], F32, name="out_sb%d" % j) for j in range(BLOCKS)]
 
         def quantise_weights(k):
-            vector_cols = VECTOR_COLS[IRREP_ORDER.index(k)]
+            position = IRREP_ORDER.index(k)
             w_codes[k] = codes_pool.tile([P, PASSES, MUL], U32, align_bytes=64, name="w_codes")
             w_scales[k] = codes_pool.tile([P, PASSES, MUL], U8, align_bytes=64, name="w_scales")
             for g in range(PASSES):
                 for c in range(COL_TILES):
                     cols = slice(c * N_TILE, (c + 1) * N_TILE)
-                    split = c * N_TILE + vector_cols
-                    grouped = grouped_pool.tile([P, N_TILE, PACK], BF16, align_bytes=64)
+                    vector_cols = VECTOR_COLS[position]
+                    if position == 0 and g * COL_TILES + c < HEAD_PIECES:
+                        vector_cols = HEAD_VECTOR_COLS
+                    grouped = grouped_pool.tile(
+                        [P, N_TILE, PACK], BF16, align_bytes=64, tag="grouped"
+                    )
                     to_view, from_view = regrouped(
-                        w_raw[(k, g)][:, :, c * N_TILE : split], grouped[:, :vector_cols, :]
+                        w_piece[(k, g, c)][:, :, :vector_cols], grouped[:, :vector_cols, :]
                     )
                     nc.vector.tensor_copy(out=to_view, in_=from_view)
                     if vector_cols < N_TILE:
                         to_view, from_view = regrouped(
-                            w_raw[(k, g)][:, :, split : (c + 1) * N_TILE],
+                            w_piece[(k, g, c)][:, :, vector_cols:],
                             grouped[:, vector_cols:, :],
                         )
                         nc.scalar.copy(out=to_view, in_=from_view)

@@ -110,30 +110,38 @@ def tile_loracuetlinear_pa_kernel(tc, x, a_lora, w_base, w_lora_b, out):
             position = IRREP_ORDER.index(k)
             w_codes[k] = codes_pool.tile([P, PASSES, MUL], U32, align_bytes=64, name="w_codes")
             w_scales[k] = codes_pool.tile([P, PASSES, MUL], U8, align_bytes=64, name="w_scales")
-            for g in range(PASSES):
-                for c in range(COL_TILES):
-                    cols = slice(c * N_TILE, (c + 1) * N_TILE)
-                    vector_cols = VECTOR_COLS[position]
-                    if position == 0 and g * COL_TILES + c < HEAD_PIECES:
-                        vector_cols = HEAD_VECTOR_COLS
-                    grouped = grouped_pool.tile(
-                        [P, N_TILE, PACK], BF16, align_bytes=64, tag="grouped"
-                    )
+            grouped_piece = {}
+
+            def regroup(g, c):
+                vector_cols = VECTOR_COLS[position]
+                if position == 0 and g * COL_TILES + c < HEAD_PIECES:
+                    vector_cols = HEAD_VECTOR_COLS
+                grouped = grouped_pool.tile([P, N_TILE, PACK], BF16, align_bytes=64, tag="grouped")
+                to_view, from_view = regrouped(
+                    w_piece[(k, g, c)][:, :, :vector_cols], grouped[:, :vector_cols, :]
+                )
+                nc.vector.tensor_copy(out=to_view, in_=from_view)
+                if vector_cols < N_TILE:
                     to_view, from_view = regrouped(
-                        w_piece[(k, g, c)][:, :, :vector_cols], grouped[:, :vector_cols, :]
+                        w_piece[(k, g, c)][:, :, vector_cols:], grouped[:, vector_cols:, :]
                     )
-                    nc.vector.tensor_copy(out=to_view, in_=from_view)
-                    if vector_cols < N_TILE:
-                        to_view, from_view = regrouped(
-                            w_piece[(k, g, c)][:, :, vector_cols:],
-                            grouped[:, vector_cols:, :],
-                        )
-                        nc.scalar.copy(out=to_view, in_=from_view)
-                    nc.vector.quantize_mx(
-                        out=w_codes[k][:, g, cols].bitcast(FP8X4),
-                        scales=w_scales[k][:, g, cols],
-                        in_=grouped[:].rearrange("p c t -> p (c t)"),
-                    )
+                    nc.scalar.copy(out=to_view, in_=from_view)
+                grouped_piece[(g, c)] = grouped
+
+            def quantise(g, c):
+                cols = slice(c * N_TILE, (c + 1) * N_TILE)
+                nc.vector.quantize_mx(
+                    out=w_codes[k][:, g, cols].bitcast(FP8X4),
+                    scales=w_scales[k][:, g, cols],
+                    in_=grouped_piece[(g, c)][:].rearrange("p c t -> p (c t)"),
+                )
+
+            pieces = [(g, c) for g in range(PASSES) for c in range(COL_TILES)]
+            regroup(*pieces[0])
+            for i, piece in enumerate(pieces):
+                if i + 1 < len(pieces):
+                    regroup(*pieces[i + 1])
+                quantise(*piece)
 
         def lora_products(k):
             first, blocks = FIRST_BLOCK[k], COMPONENTS[k]

@@ -32,7 +32,7 @@ IRREP_ORDER = (2, 1, 0)
 BASE_FACTOR = 1.0 / math.sqrt(MUL)
 LORA_FACTOR = 2.0 / math.sqrt(RANK)
 
-VECTOR_COLS = (N_TILE, 176, 176)
+VECTOR_COLS = (N_TILE, 176, 128)
 HEAD_PIECES = 2
 HEAD_VECTOR_COLS = 336
 
@@ -112,31 +112,32 @@ def tile_loracuetlinear_pa_kernel(tc, x, a_lora, w_base, w_lora_b, out):
             w_scales[k] = codes_pool.tile([P, PASSES, MUL], U8, align_bytes=64, name="w_scales")
             grouped_piece = {}
 
-            def regroup(g, c):
-                vector_cols = VECTOR_COLS[position]
-                if position == 0 and g * COL_TILES + c < HEAD_PIECES:
+            def regroup(g, first, n):
+                vector_cols = VECTOR_COLS[position] * n // N_TILE
+                if position == 0 and g == 0 and first < HEAD_PIECES * N_TILE:
                     vector_cols = HEAD_VECTOR_COLS
+                rows = w_piece[(k, g, first // N_TILE)][:, :, first % N_TILE : first % N_TILE + n]
                 grouped = grouped_pool.tile([P, N_TILE, PACK], BF16, align_bytes=64, tag="grouped")
-                to_view, from_view = regrouped(
-                    w_piece[(k, g, c)][:, :, :vector_cols], grouped[:, :vector_cols, :]
-                )
+                to_view, from_view = regrouped(rows[:, :, :vector_cols], grouped[:, :vector_cols, :])
                 nc.vector.tensor_copy(out=to_view, in_=from_view)
-                if vector_cols < N_TILE:
+                if vector_cols < n:
                     to_view, from_view = regrouped(
-                        w_piece[(k, g, c)][:, :, vector_cols:], grouped[:, vector_cols:, :]
+                        rows[:, :, vector_cols:], grouped[:, vector_cols:n, :]
                     )
                     nc.scalar.copy(out=to_view, in_=from_view)
-                grouped_piece[(g, c)] = grouped
+                grouped_piece[(g, first)] = grouped
 
-            def quantise(g, c):
-                cols = slice(c * N_TILE, (c + 1) * N_TILE)
+            def quantise(g, first, n):
                 nc.vector.quantize_mx(
-                    out=w_codes[k][:, g, cols].bitcast(FP8X4),
-                    scales=w_scales[k][:, g, cols],
-                    in_=grouped_piece[(g, c)][:].rearrange("p c t -> p (c t)"),
+                    out=w_codes[k][:, g, first : first + n].bitcast(FP8X4),
+                    scales=w_scales[k][:, g, first : first + n],
+                    in_=grouped_piece[(g, first)][:, :n, :].rearrange("p c t -> p (c t)"),
                 )
 
-            pieces = [(g, c) for g in range(PASSES) for c in range(COL_TILES)]
+            pieces = [(g, c * N_TILE, N_TILE) for g in range(PASSES) for c in range(COL_TILES)]
+            if position == len(IRREP_ORDER) - 1:
+                g, first, n = pieces[-1]
+                pieces[-1:] = [(g, first, n // 2), (g, first + n // 2, n // 2)]
             regroup(*pieces[0])
             for i, piece in enumerate(pieces):
                 if i + 1 < len(pieces):
@@ -196,13 +197,17 @@ def tile_loracuetlinear_pa_kernel(tc, x, a_lora, w_base, w_lora_b, out):
         def finish_blocks(k):
             for i in range(COMPONENTS[k]):
                 j = FIRST_BLOCK[k] + i
-                for c in range(COL_TILES):
-                    cols = slice(c * N_TILE, (c + 1) * N_TILE)
+                ranges = [(c * N_TILE, N_TILE) for c in range(COL_TILES)]
+                if k == IRREP_ORDER[-1]:
+                    first, n = ranges[-1]
+                    ranges[-1:] = [(first, n // 2), (first + n // 2, n // 2)]
+                for first, n in ranges:
+                    cols = slice(first, first + n)
                     acc = product_pool.tile([P, N_TILE], F32, tag="product")
                     for g in range(PASSES):
                         at = (j * PASSES + g) * NODES
                         nc.tensor.matmul_mx(
-                            out=acc[:],
+                            out=acc[:, :n],
                             lhsT=x_codes[:, at : at + NODES].bitcast(FP8X4),
                             lhsT_scale=x_scales[:, at : at + NODES],
                             rhs=w_codes[k][:, g, cols].bitcast(FP8X4),
@@ -212,15 +217,14 @@ def tile_loracuetlinear_pa_kernel(tc, x, a_lora, w_base, w_lora_b, out):
                         )
                     nc.vector.scalar_tensor_tensor(
                         out=out_sb[j][:, cols],
-                        in0=acc[:],
+                        in0=acc[:, :n],
                         scalar=BASE_FACTOR,
                         in1=out_sb[j][:, cols],
                         op0=MULT,
                         op1=ADD,
                     )
                     nc.sync.dma_start(
-                        out=out[:, j * MUL + c * N_TILE : j * MUL + (c + 1) * N_TILE],
-                        in_=out_sb[j][:, cols],
+                        out=out[:, j * MUL + first : j * MUL + first + n], in_=out_sb[j][:, cols]
                     )
 
         first_irrep, second_irrep, last_irrep = IRREP_ORDER

@@ -41,8 +41,8 @@ FLOPS = 2 * NODES * BLOCKS * MUL * (MUL + RANK)
 
 def regrouped(rows, grouped):
     return (
-        grouped.rearrange("p (c i) t -> p c t i", i=4),
-        rows.rearrange("p t (c i) -> p c t i", i=4),
+        grouped.rearrange("p (c i) t -> p c t i", i=8),
+        rows.rearrange("p t (c i) -> p c t i", i=8),
     )
 
 

@@ -223,9 +223,13 @@ def tile_loracuetlinear_pa_kernel(tc, x, a_lora, w_base, w_lora_b, out):
                         op0=MULT,
                         op1=ADD,
                     )
-                    nc.sync.dma_start(
-                        out=out[:, j * MUL + first : j * MUL + first + n], in_=out_sb[j][:, cols]
-                    )
+                    if k == IRREP_ORDER[-1]:
+                        nc.sync.dma_start(
+                            out=out[:, j * MUL + first : j * MUL + first + n],
+                            in_=out_sb[j][:, cols],
+                        )
+                if k != IRREP_ORDER[-1]:
+                    nc.sync.dma_start(out=out[:, j * MUL : (j + 1) * MUL], in_=out_sb[j][:])
 
         first_irrep, second_irrep, last_irrep = IRREP_ORDER
         quantise_weights(first_irrep)

import math
from contextlib import ExitStack

import concourse.mybir as mybir
from concourse.masks import make_identity

F32 = mybir.dt.float32
BF16 = mybir.dt.bfloat16
U32 = mybir.dt.uint32
U8 = mybir.dt.uint8
FP8X4 = mybir.dt.float8_e4m3fn_x4
MULT = mybir.AluOpType.mult
ADD = mybir.AluOpType.add

P = 128
PACK = 4
K_PASS = P * PACK
N_TILE = 512

NODES = 128
MUL = 1536
RANK = 128
COMPONENTS = (1, 3, 5)
FIRST_BLOCK = (0, 1, 4)
BLOCKS = sum(COMPONENTS)
PASSES = MUL // K_PASS
COL_TILES = MUL // N_TILE
WORDS_PASS = K_PASS // 2

IRREP_ORDER = (2, 1, 0)

BASE_FACTOR = 1.0 / math.sqrt(MUL)
LORA_FACTOR = 2.0 / math.sqrt(RANK)

VECTOR_COLS = (N_TILE, 176, 128)
HEAD_PIECES = 2
HEAD_VECTOR_COLS = 336

FLOPS = 2 * NODES * BLOCKS * MUL * (MUL + RANK)


def regrouped(rows, grouped):
    return (
        grouped.rearrange("p (c i) t -> p c t i", i=8),
        rows.rearrange("p t (c i) -> p c t i", i=8),
    )


def tile_loracuetlinear_pa_kernel(tc, x, a_lora, w_base, w_lora_b, out):
    nc = tc.nc
    with ExitStack() as ctx:
        resident = ctx.enter_context(tc.tile_pool(name="resident", bufs=1))
        raw_pool = ctx.enter_context(tc.tile_pool(name="raw", bufs=4))
        grouped_pool = ctx.enter_context(tc.tile_pool(name="grouped", bufs=6))
        x_grouped_pool = ctx.enter_context(tc.tile_pool(name="x_grouped", bufs=3))
        codes_pool = ctx.enter_context(tc.tile_pool(name="codes", bufs=2))
        transposed_pool = ctx.enter_context(tc.psum_pool(name="transposed", bufs=2))
        product_pool = ctx.enter_context(tc.psum_pool(name="product", bufs=6))

        ident_f32 = resident.tile([P, P], F32)
        make_identity(nc, ident_f32[:])
        ident_bf16 = resident.tile([P, P], BF16)
        make_identity(nc, ident_bf16[:])

        a_raw = resident.tile([P, BLOCKS * RANK], BF16)

        lora_w = {}
        x_raw = {}
        side_loads = []
        for k in IRREP_ORDER:
            lora_w[k] = resident.tile([P, MUL], BF16, name="lora_w%d" % k)
            side_loads.append((lora_w[k], w_lora_b[k, :, :]))
        for k in IRREP_ORDER:
            first, blocks = FIRST_BLOCK[k], COMPONENTS[k]
            x_raw[k] = resident.tile([P, blocks * MUL], BF16, name="x_raw%d" % k)
            side_loads.append((x_raw[k], x[:, first * MUL : (first + blocks) * MUL]))

        w_piece = {}
        for n, (k, g) in enumerate([(k, g) for k in IRREP_ORDER for g in range(PASSES)]):
            rows = w_base[k, g * K_PASS : (g + 1) * K_PASS, :].rearrange("(p t) c -> p t c", t=PACK)
            if n == 0:
                for c in range(COL_TILES):
                    if c == HEAD_PIECES:
                        nc.sync.dma_start(out=a_raw[:], in_=a_lora[:, :])
                        side_tile, side_source = side_loads[0]
                        nc.sync.dma_start(out=side_tile[:], in_=side_source)
                    first_raw = grouped_pool.tile(
                        [P, PACK, N_TILE], BF16, align_bytes=64, tag="grouped"
                    )
                    nc.sync.dma_start(
                        out=first_raw[:], in_=rows[:, :, c * N_TILE : (c + 1) * N_TILE]
                    )
                    w_piece[(k, g, c)] = first_raw[:]
            else:
                if n < len(side_loads):
                    side_tile, side_source = side_loads[n]
                    nc.sync.dma_start(out=side_tile[:], in_=side_source)
                w_raw = raw_pool.tile([P, PACK, MUL], BF16)
                nc.sync.dma_start(out=w_raw[:], in_=rows)
                for c in range(COL_TILES):
                    w_piece[(k, g, c)] = w_raw[:, :, c * N_TILE : (c + 1) * N_TILE]

        x_codes = resident.tile([P, BLOCKS * PASSES * NODES], U32, align_bytes=64)
        x_scales = resident.tile([P, BLOCKS * PASSES * NODES], U8, align_bytes=64)
        w_codes = {}
        w_scales = {}
        out_sb = [resident.tile([P, MUL], F32, name="out_sb%d" % j) for j in range(BLOCKS)]

        def quantise_weights(k):
            position = IRREP_ORDER.index(k)
            w_codes[k] = codes_pool.tile([P, PASSES, MUL], U32, align_bytes=64, name="w_codes")
            w_scales[k] = codes_pool.tile([P, PASSES, MUL], U8, align_bytes=64, name="w_scales")
            grouped_piece = {}

            def regroup(g, first, n):
                vector_cols = VECTOR_COLS[position] * n // N_TILE
                if position == 0 and g == 0 and first < HEAD_PIECES * N_TILE:
                    vector_cols = HEAD_VECTOR_COLS
                rows = w_piece[(k, g, first // N_TILE)][:, :, first % N_TILE : first % N_TILE + n]
                grouped = grouped_pool.tile([P, N_TILE, PACK], BF16, align_bytes=64, tag="grouped")
                to_view, from_view = regrouped(rows[:, :, :vector_cols], grouped[:, :vector_cols, :])
                nc.vector.tensor_copy(out=to_view, in_=from_view)
                if vector_cols < n:
                    to_view, from_view = regrouped(
                        rows[:, :, vector_cols:], grouped[:, vector_cols:n, :]
                    )
                    nc.scalar.copy(out=to_view, in_=from_view)
                grouped_piece[(g, first)] = grouped

            def quantise(g, first, n):
                nc.vector.quantize_mx(
                    out=w_codes[k][:, g, first : first + n].bitcast(FP8X4),
                    scales=w_scales[k][:, g, first : first + n],
                    in_=grouped_piece[(g, first)][:, :n, :].rearrange("p c t -> p (c t)"),
                )

            pieces = [(g, c * N_TILE, N_TILE) for g in range(PASSES) for c in range(COL_TILES)]
            if position == len(IRREP_ORDER) - 1:
                g, first, n = pieces[-1]
                pieces[-1:] = [(g, first, n // 2), (g, first + n // 2, n // 2)]
            regroup(*pieces[0])
            for i, piece in enumerate(pieces):
                if i + 1 < len(pieces):
                    regroup(*pieces[i + 1])
                quantise(*piece)

        def lora_products(k):
            first, blocks = FIRST_BLOCK[k], COMPONENTS[k]
            a_t_psum = transposed_pool.tile([P, blocks, NODES], BF16, tag="transposed")
            for i in range(blocks):
                j = first + i
                nc.tensor.transpose(
                    a_t_psum[:, i, :], a_raw[:, j * RANK : (j + 1) * RANK], ident_bf16[:]
                )
            a_t = resident.tile([P, blocks, NODES], BF16, name="a_t%d" % k)
            nc.scalar.copy(out=a_t[:], in_=a_t_psum[:])
            for i in range(blocks):
                for c in range(COL_TILES):
                    cols = slice(c * N_TILE, (c + 1) * N_TILE)
                    lora_psum = product_pool.tile([P, N_TILE], F32, tag="product")
                    nc.tensor.matmul(
                        out=lora_psum[:],
                        lhsT=a_t[:, i, :],
                        rhs=lora_w[k][:, cols],
                        start=True,
                        stop=True,
                    )
                    nc.scalar.mul(
                        out=out_sb[first + i][:, cols], in_=lora_psum[:], mul=LORA_FACTOR
                    )

        def quantise_x(k):
            first, blocks = FIRST_BLOCK[k], COMPONENTS[k]
            words = x_raw[k][:].bitcast(F32)
            x_passes = blocks * PASSES
            for q in range(0, x_passes, 2):
                n = min(2, x_passes - q)
                x_t = transposed_pool.tile([P, 2, 2, NODES], F32, tag="transposed")
                for i in range(n):
                    pass_words = words[:, (q + i) * WORDS_PASS : (q + i + 1) * WORDS_PASS]
                    halves = pass_words.rearrange("n (p u) -> n u p", u=2)
                    for u in range(2):
                        nc.tensor.transpose(x_t[:, i, u, :], halves[:, u, :], ident_f32[:])
                x_grouped = x_grouped_pool.tile([P, 2 * NODES * PACK], BF16, align_bytes=64)
                filled = x_grouped[:, : n * NODES * PACK]
                nc.scalar.copy(
                    out=filled.bitcast(F32).rearrange("p (i m u) -> p i m u", i=n, u=2),
                    in_=x_t[:, :n, :, :].rearrange("p i u m -> p i m u"),
                )
                at = (first * PASSES + q) * NODES
                nc.vector.quantize_mx(
                    out=x_codes[:, at : at + n * NODES].bitcast(FP8X4),
                    scales=x_scales[:, at : at + n * NODES],
                    in_=filled,
                )

        def finish_blocks(k):
            for i in range(COMPONENTS[k]):
                j = FIRST_BLOCK[k] + i
                ranges = [(c * N_TILE, N_TILE) for c in range(COL_TILES)]
                if k == IRREP_ORDER[-1]:
                    first, n = ranges[-1]
                    ranges[-1:] = [(first, n // 2), (first + n // 2, n // 2)]
                for first, n in ranges:
                    cols = slice(first, first + n)
                    acc = product_pool.tile([P, N_TILE], F32, tag="product")
                    for g in range(PASSES):
                        at = (j * PASSES + g) * NODES
                        nc.tensor.matmul_mx(
                            out=acc[:, :n],
                            lhsT=x_codes[:, at : at + NODES].bitcast(FP8X4),
                            lhsT_scale=x_scales[:, at : at + NODES],
                            rhs=w_codes[k][:, g, cols].bitcast(FP8X4),
                            rhs_scale=w_scales[k][:, g, cols],
                            start=(g == 0),
                            stop=(g == PASSES - 1),
                        )
                    nc.vector.scalar_tensor_tensor(
                        out=out_sb[j][:, cols],
                        in0=acc[:, :n],
                        scalar=BASE_FACTOR,
                        in1=out_sb[j][:, cols],
                        op0=MULT,
                        op1=ADD,
                    )
                    if k == IRREP_ORDER[-1]:
                        nc.sync.dma_start(
                            out=out[:, j * MUL + first : j * MUL + first + n],
                            in_=out_sb[j][:, cols],
                        )
                if k != IRREP_ORDER[-1]:
                    nc.sync.dma_start(out=out[:, j * MUL : (j + 1) * MUL], in_=out_sb[j][:])

        first_irrep, second_irrep, last_irrep = IRREP_ORDER
        quantise_weights(first_irrep)
        for k in IRREP_ORDER:
            lora_products(k)
        quantise_x(first_irrep)
        quantise_weights(second_irrep)
        finish_blocks(first_irrep)
        quantise_x(second_irrep)
        quantise_x(last_irrep)
        quantise_weights(last_irrep)
        finish_blocks(second_irrep)
        finish_blocks(last_irrep)
